import numpy as np
import ml_dtypes


def mxq(x, axis, fmt="e4m3"):
    dtype, down = {"e4m3": (ml_dtypes.float8_e4m3fn, 7), "e5m2": (ml_dtypes.float8_e5m2, 14)}[fmt]
    v = np.moveaxis(np.asarray(x, np.float32).astype(ml_dtypes.bfloat16).astype(np.float64), axis, -1)
    blocks = v.reshape(v.shape[:-1] + (-1, 32))
    amax = np.abs(blocks).max(-1, keepdims=True)
    byte = np.maximum(np.where(amax > 0, np.frexp(amax)[1] - 1 + 127, 0) - down, 1)
    scale = np.exp2(byte - 127.0)
    codes = (blocks / scale).astype(np.float32).astype(dtype).astype(np.float64)
    return np.moveaxis((codes * scale).reshape(v.shape), -1, axis)


WIDE = False


def mx_kscale(k):
    if not WIDE:
        return np.ones(k)
    levels = np.array([10, -10, 5, -5, 0])
    a = np.random.permutation(np.resize(levels, k // 512 * 4)).reshape(k // 512, 4)
    idx = np.arange(k)
    return np.exp2(a[idx // 512, idx % 128 // 32])


BF16 = ml_dtypes.bfloat16


def bf(x):
    return np.asarray(x, np.float32).astype(BF16)


def f64(x):
    return np.asarray(x).astype(np.float64)


E2M1 = np.array([0.0, 0.5, 1.0, 1.5, 2.0, 3.0, 4.0, 6.0, -0.0, -0.5, -1.0, -1.5, -2.0, -3.0, -4.0, -6.0])


def pack_weight(w, fmt):
    k, n = w.shape
    w = f64(bf(w)).reshape(k // 32, 32, n)
    amax = np.abs(w).max(1)
    if fmt == "e4m3":
        byte = np.frexp(amax)[1] - 1 + 127 - 7
    else:
        mant, ex = np.frexp(amax / 6.0)
        byte = np.where(mant > 0.5, ex, ex - 1) + 127
    byte = np.clip(np.where(amax > 0, byte, 1), 1, 254)
    scaled = (w * np.exp2(127.0 - byte)[:, None, :]).reshape(k, n).astype(np.float32)
    by_word = np.ascontiguousarray(scaled.reshape(k // 512, 128, 4, n).transpose(0, 1, 3, 2))
    if fmt == "e4m3":
        words = by_word.astype(ml_dtypes.float8_e4m3fn).view(np.uint8)
    else:
        c = by_word.astype(ml_dtypes.float4_e2m1fn).view(np.uint8) & 0xF
        words = c[..., 0::2] | (c[..., 1::2] << 4)
    return np.ascontiguousarray(words), np.ascontiguousarray(byte.astype(np.uint8).reshape(k // 512, 16, n))


def unpack_weight(words, scales, fmt):
    g, p, n, _ = words.shape
    if fmt == "e4m3":
        vals = np.ascontiguousarray(words).view(ml_dtypes.float8_e4m3fn).astype(np.float64)
    else:
        nib = np.empty((g, p, n, 4), np.uint8)
        nib[..., 0::2] = words & 0xF
        nib[..., 1::2] = words >> 4
        vals = E2M1[nib]
    vals = vals * np.repeat(np.exp2(scales.astype(np.float64) - 127.0), 8, axis=1)[..., None]
    return vals.transpose(0, 1, 3, 2).reshape(g * 512, n)


NB, D1, KB, P, Q, LB, S = 4, 256, 8, 512, 512, 8, 512
D2 = KB * P
R = KB * Q // LB
DO = S * LB


def _blockdiag_butterfly_multiply(x, w1, w2):
    B, n = x.shape
    k, q, p = w1.shape
    l, s, r = w2.shape
    x_r = x.reshape(B, k, p).transpose(1, 0, 2)
    out1 = mxq(x_r, 2, "e4m3") @ w1.transpose(0, 2, 1)
    out1 = out1.transpose(1, 0, 2).reshape(B, r, l).transpose(2, 0, 1)
    out2 = mxq(out1, 2, "e4m3") @ w2.transpose(0, 2, 1)
    return out2.transpose(1, 2, 0).reshape(B, s * l)


def setup_inputs():
    s = mx_kscale(P)
    t = mx_kscale(R)
    tf = np.repeat(t, LB).reshape(KB, Q)
    x = bf(np.random.standard_normal((NB, D1, D2)) * np.tile(s, KB))
    fl = np.random.standard_normal((KB, Q, P)) / np.sqrt(P) / s * tf[:, :, None]
    fl_words, fl_scales = pack_weight(fl.swapaxes(1, 2).reshape(-1, Q), "e4m3")
    fr = np.random.standard_normal((LB, S, R)) / np.sqrt(R) / t
    fr_words, fr_scales = pack_weight(fr.swapaxes(1, 2).reshape(-1, S), "e4m3")
    bias = bf(np.random.standard_normal(DO) * 0.5)
    return {"x": x,
            "factorL_words": fl_words, "factorL_scales": fl_scales,
            "factorR_words": fr_words, "factorR_scales": fr_scales,
            "bias": bias}


def reference(x, factorL_words, factorL_scales, factorR_words, factorR_scales, bias):
    b, d1, d2 = x.shape
    w1 = unpack_weight(factorL_words, factorL_scales, "e4m3").reshape(KB, P, Q).swapaxes(1, 2)
    w2 = unpack_weight(factorR_words, factorR_scales, "e4m3").reshape(LB, R, S).swapaxes(1, 2)
    out = _blockdiag_butterfly_multiply(f64(x).reshape(-1, d2), w1, w2)
    out = out.reshape(b, d1, -1)
    return out + f64(bias)

@@ -1,0 +1,172 @@
+from contextlib import ExitStack
+
+import concourse.mybir as mybir
+from concourse.masks import make_identity
+
+F32 = mybir.dt.float32
+BF16 = mybir.dt.bfloat16
+I32 = mybir.dt.int32
+U32 = mybir.dt.uint32
+U8 = mybir.dt.uint8
+FP8X4 = mybir.dt.float8_e4m3fn_x4
+
+P = 128
+PACK = 4
+BLOCKS = 8
+BLOCK = P * PACK
+TOKENS = 1024
+WIDTH = BLOCKS * BLOCK
+TILES = TOKENS // P
+PSUM_BANKS = 8
+QUADRANTS = 4
+HALF = BLOCKS // 2
+
+FLOPS = 2 * 2 * TOKENS * BLOCKS * BLOCK * BLOCK
+
+
+def tile_butterflyblocksparselinear_e_kernel(
+    tc, x, factorL_words, factorL_scales, factorR_words, factorR_scales, bias, out
+):
+    nc = tc.nc
+    x_rows = x.flatten_outer_dims()
+    out_rows = out.flatten_outer_dims()
+
+    with ExitStack() as ctx:
+        keep = ctx.enter_context(tc.tile_pool(name="keep", bufs=1))
+        inputs = ctx.enter_context(tc.tile_pool(name="inputs", bufs=TILES))
+        work = ctx.enter_context(tc.tile_pool(name="work", bufs=2))
+        results = ctx.enter_context(tc.tile_pool(name="results", bufs=4))
+        psum = ctx.enter_context(tc.psum_pool(name="psum", bufs=PSUM_BANKS))
+        ctx.enter_context(tc.manual_schedule())
+
+        identity = keep.tile([P, P], F32, name="identity")
+        make_identity(nc, identity[:])
+
+        def load_tokens(i):
+            tokens = inputs.tile([P, WIDTH], BF16, name="tokens")
+            nc.sync.dma_start(out=tokens[:], in_=x_rows[P * i : P * (i + 1), :])
+            return tokens
+
+        def load_factor(words, scales, label):
+            codes = keep.tile([P, BLOCKS, PACK * BLOCK], U8, name=label + "_codes", align_bytes=64)
+            planes = keep.tile([P, BLOCKS, BLOCK], U8, name=label + "_planes", align_bytes=64)
+            nc.vector.memset(planes[:].bitcast(I32), 0)
+            scale_words = scales.bitcast(I32)
+            for quadrant in range(QUADRANTS):
+                nc.sync.dma_start(
+                    out=planes[32 * quadrant : 32 * quadrant + 4].bitcast(I32),
+                    in_=scale_words[:, 4 * quadrant : 4 * quadrant + 4, :].rearrange("e r n -> r e n"),
+                )
+            nc.sync.dma_start(
+                out=codes[:].bitcast(I32),
+                in_=words.rearrange("e p n t -> p e (n t)").bitcast(I32),
+            )
+            return codes, planes
+
+        tokens_of = {}
+        tokens_of[0] = load_tokens(0)
+        tokens_of[1] = load_tokens(1)
+        l_codes, l_planes = load_factor(factorL_words, factorL_scales, "l")
+        tokens_of[2] = load_tokens(2)
+        r_codes, r_planes = load_factor(factorR_words, factorR_scales, "r")
+        tokens_of[3] = load_tokens(3)
+        bias_rows = keep.tile([P, WIDTH], BF16, name="bias_rows")
+        nc.sync.dma_start(out=bias_rows[:], in_=bias.partition_broadcast(P))
+        bias_by_column_tile = bias_rows[:].rearrange("p (c s l) -> p c s l", s=P, l=BLOCKS)
+        for i in range(4, TILES):
+            tokens_of[i] = load_tokens(i)
+
+        def make_operand(pairs, label):
+            grouped = work.tile([P, BLOCKS, P, PACK], BF16, name=label + "_grouped", align_bytes=64)
+            codes = work.tile([P, BLOCKS, P], U32, name=label + "_codes", align_bytes=64)
+            planes = work.tile([P, BLOCKS, P], U8, name=label + "_planes", align_bytes=64)
+            grouped_words = grouped[:].bitcast(F32)
+            for two in range(BLOCKS // 2):
+                bank = psum.tile([P, BLOCK], F32, name="bank")
+                planes_of_bank = bank[:].rearrange("p (j u n) -> p j u n", j=2, u=2)
+                for j in range(2):
+                    for u in range(2):
+                        nc.tensor.transpose(planes_of_bank[:, j, u, :], pairs[:, 2 * two + j, u, :], identity[:])
+                copy = nc.vector.tensor_copy if two % 4 == 3 else nc.scalar.copy
+                copy(
+                    out=grouped_words[:, 2 * two : 2 * two + 2],
+                    in_=bank[:].rearrange("p (j u n) -> p j n u", j=2, u=2),
+                )
+            for half in range(2):
+                blocks = slice(HALF * half, HALF * (half + 1))
+                nc.vector.quantize_mx(
+                    out=codes[:, blocks, :].rearrange("p e n -> p (e n)").bitcast(FP8X4),
+                    scales=planes[:, blocks, :].rearrange("p e n -> p (e n)"),
+                    in_=grouped[:, blocks].rearrange("p e n t -> p (e n t)"),
+                )
+            return codes, planes
+
+        def first_product(operand, hidden, k):
+            codes, planes = operand
+            bank = psum.tile([P, BLOCK], F32, name="bank")
+            nc.tensor.matmul_mx(
+                out=bank[:],
+                lhsT=codes[:, k, :].bitcast(FP8X4),
+                lhsT_scale=planes[:, k, :],
+                rhs=l_codes[:, k, :].bitcast(FP8X4),
+                rhs_scale=l_planes[:, k, :],
+                start=True,
+                stop=True,
+            )
+            source = bank[:].rearrange("p (a u e l) -> p u l a e", u=2, e=2, l=BLOCKS)
+            target = hidden[:].rearrange("p l u (c e) -> p u l c e", e=2)
+            for u in range(2):
+                nc.scalar.copy(out=target[:, u, :, 16 * k : 16 * (k + 1), :], in_=source[:, u])
+
+        def second_product(operand, column_tile, half, result):
+            codes, planes = operand
+            bank = psum.tile([P, BLOCK], F32, name="bank")
+            by_block = bank[:].rearrange("p (j s) -> p j s", j=HALF)
+            for j in range(HALF):
+                l = HALF * half + j
+                nc.tensor.matmul_mx(
+                    out=by_block[:, j, :],
+                    lhsT=codes[:, l, :].bitcast(FP8X4),
+                    lhsT_scale=planes[:, l, :],
+                    rhs=r_codes[:, l, PACK * P * column_tile : PACK * P * (column_tile + 1)].bitcast(FP8X4),
+                    rhs_scale=r_planes[:, l, P * column_tile : P * (column_tile + 1)],
+                    start=True,
+                    stop=True,
+                )
+            these = slice(HALF * half, HALF * (half + 1))
+            nc.vector.tensor_tensor(
+                out=result[:, :, these],
+                in0=bank[:].rearrange("p (j s) -> p s j", j=HALF),
+                in1=bias_by_column_tile[:, column_tile, :, these],
+                op=mybir.AluOpType.add,
+            )
+
+        x_operand = {}
+        hidden_of = {}
+        g_operand = {}
+        for step in range(TILES + 3):
+            if step < TILES:
+                x_pairs = tokens_of[step][:].bitcast(F32).rearrange("p (e c u) -> p e u c", e=BLOCKS, u=2)
+                x_operand[step] = make_operand(x_pairs, "x")
+            if 0 <= step - 2 < TILES:
+                g_operand[step - 2] = make_operand(hidden_of[step - 2][:].bitcast(F32), "g")
+            first = step - 1
+            second = step - 3
+            if 0 <= first < TILES:
+                hidden_of[first] = work.tile([P, BLOCKS, 2, 2 * P], BF16, name="hidden")
+            for column_tile in range(BLOCK // P):
+                if 0 <= second < TILES:
+                    result = results.tile([P, P, BLOCKS], F32, name="result")
+                for half in range(2):
+                    if 0 <= first < TILES:
+                        first_product(x_operand[first], hidden_of[first], 2 * column_tile + half)
+                    if 0 <= second < TILES:
+                        second_product(g_operand[second], column_tile, half, result)
+                if 0 <= second < TILES:
+                    nc.sync.dma_start(
+                        out=out_rows[
+                            P * second : P * (second + 1),
+                            BLOCKS * P * column_tile : BLOCKS * P * (column_tile + 1),
+                        ],
+                        in_=result[:].rearrange("p s l -> p (s l)"),
+                    )

@@ -21,6 +21,11 @@ PSUM_BANKS = 8
 QUADRANTS = 4
 HALF = BLOCKS // 2
 
+FIRST_PRODUCT_LAG = 1
+HIDDEN_TRANSPOSE_LAG = 3
+SECOND_PRODUCT_LAG = 4
+ROUNDS = 2 * TILES + SECOND_PRODUCT_LAG
+
 FLOPS = 2 * 2 * TOKENS * BLOCKS * BLOCK * BLOCK
 
 
@@ -35,20 +40,19 @@ def tile_butterflyblocksparselinear_e_kernel(
         keep = ctx.enter_context(tc.tile_pool(name="keep", bufs=1))
         inputs = ctx.enter_context(tc.tile_pool(name="inputs", bufs=TILES))
         work = ctx.enter_context(tc.tile_pool(name="work", bufs=2))
-        results = ctx.enter_context(tc.tile_pool(name="results", bufs=4))
         psum = ctx.enter_context(tc.psum_pool(name="psum", bufs=PSUM_BANKS))
         ctx.enter_context(tc.manual_schedule())
 
         identity = keep.tile([P, P], F32, name="identity")
         make_identity(nc, identity[:])
 
+
         def load_tokens(i):
             tokens = inputs.tile([P, WIDTH], BF16, name="tokens")
             nc.sync.dma_start(out=tokens[:], in_=x_rows[P * i : P * (i + 1), :])
             return tokens
 
-        def load_factor(words, scales, label):
-            codes = keep.tile([P, BLOCKS, PACK * BLOCK], U8, name=label + "_codes", align_bytes=64)
+        def load_planes(scales, label):
             planes = keep.tile([P, BLOCKS, BLOCK], U8, name=label + "_planes", align_bytes=64)
             nc.vector.memset(planes[:].bitcast(I32), 0)
             scale_words = scales.bitcast(I32)
@@ -57,57 +61,69 @@ def tile_butterflyblocksparselinear_e_kernel(
                     out=planes[32 * quadrant : 32 * quadrant + 4].bitcast(I32),
                     in_=scale_words[:, 4 * quadrant : 4 * quadrant + 4, :].rearrange("e r n -> r e n"),
                 )
-            nc.sync.dma_start(
-                out=codes[:].bitcast(I32),
-                in_=words.rearrange("e p n t -> p e (n t)").bitcast(I32),
-            )
-            return codes, planes
+            return planes
 
+        def load_codes(codes, words, half):
+            blocks = slice(HALF * half, HALF * (half + 1))
+            nc.sync.dma_start(
+                out=codes[:, blocks, :].bitcast(I32),
+                in_=words[blocks].rearrange("e p n t -> p e (n t)").bitcast(I32),
+            )
+
+        l_codes = keep.tile([P, BLOCKS, PACK * BLOCK], U8, name="l_codes", align_bytes=64)
+        r_codes = keep.tile([P, BLOCKS, PACK * BLOCK], U8, name="r_codes", align_bytes=64)
+        bias_rows = keep.tile([P, WIDTH], BF16, name="bias_rows")
         tokens_of = {}
         tokens_of[0] = load_tokens(0)
+        l_planes = load_planes(factorL_scales, "l")
+        load_codes(l_codes, factorL_words, 0)
         tokens_of[1] = load_tokens(1)
-        l_codes, l_planes = load_factor(factorL_words, factorL_scales, "l")
+        load_codes(l_codes, factorL_words, 1)
         tokens_of[2] = load_tokens(2)
-        r_codes, r_planes = load_factor(factorR_words, factorR_scales, "r")
-        tokens_of[3] = load_tokens(3)
-        bias_rows = keep.tile([P, WIDTH], BF16, name="bias_rows")
+        r_planes = load_planes(factorR_scales, "r")
+        load_codes(r_codes, factorR_words, 0)
         nc.sync.dma_start(out=bias_rows[:], in_=bias.partition_broadcast(P))
-        bias_by_column_tile = bias_rows[:].rearrange("p (c s l) -> p c s l", s=P, l=BLOCKS)
-        for i in range(4, TILES):
+        load_codes(r_codes, factorR_words, 1)
+        for i in range(3, TILES):
             tokens_of[i] = load_tokens(i)
+        bias_by_column_tile = bias_rows[:].rearrange("p (c s l) -> p c s l", s=P, l=BLOCKS)
 
-        def make_operand(pairs, label):
+
+        def new_operand(label):
             grouped = work.tile([P, BLOCKS, P, PACK], BF16, name=label + "_grouped", align_bytes=64)
             codes = work.tile([P, BLOCKS, P], U32, name=label + "_codes", align_bytes=64)
             planes = work.tile([P, BLOCKS, P], U8, name=label + "_planes", align_bytes=64)
-            grouped_words = grouped[:].bitcast(F32)
-            for two in range(BLOCKS // 2):
+            return grouped, codes, planes
+
+        def transpose_half(pairs, operand, half, copies):
+            grouped_words = operand[0][:].bitcast(F32)
+            for b in range(HALF // 2):
+                first_block = HALF * half + 2 * b
                 bank = psum.tile([P, BLOCK], F32, name="bank")
-                planes_of_bank = bank[:].rearrange("p (j u n) -> p j u n", j=2, u=2)
+                by_plane = bank[:].rearrange("p (j u n) -> p j u n", j=2, u=2)
                 for j in range(2):
                     for u in range(2):
-                        nc.tensor.transpose(planes_of_bank[:, j, u, :], pairs[:, 2 * two + j, u, :], identity[:])
-                copy = nc.vector.tensor_copy if two % 4 == 3 else nc.scalar.copy
-                copy(
-                    out=grouped_words[:, 2 * two : 2 * two + 2],
+                        nc.tensor.transpose(by_plane[:, j, u, :], pairs[:, first_block + j, u, :], identity[:])
+                copies[b](
+                    out=grouped_words[:, first_block : first_block + 2],
                     in_=bank[:].rearrange("p (j u n) -> p j n u", j=2, u=2),
                 )
-            for half in range(2):
-                blocks = slice(HALF * half, HALF * (half + 1))
-                nc.vector.quantize_mx(
-                    out=codes[:, blocks, :].rearrange("p e n -> p (e n)").bitcast(FP8X4),
-                    scales=planes[:, blocks, :].rearrange("p e n -> p (e n)"),
-                    in_=grouped[:, blocks].rearrange("p e n t -> p (e n t)"),
-                )
-            return codes, planes
 
-        def first_product(operand, hidden, k):
-            codes, planes = operand
+        def quantise_half(operand, half):
+            grouped, codes, planes = operand
+            blocks = slice(HALF * half, HALF * (half + 1))
+            nc.vector.quantize_mx(
+                out=codes[:, blocks, :].rearrange("p e n -> p (e n)").bitcast(FP8X4),
+                scales=planes[:, blocks, :].rearrange("p e n -> p (e n)"),
+                in_=grouped[:, blocks].rearrange("p e n t -> p (e n t)"),
+            )
+
+        def first_product(operand, hidden, k, copy):
             bank = psum.tile([P, BLOCK], F32, name="bank")
             nc.tensor.matmul_mx(
                 out=bank[:],
-                lhsT=codes[:, k, :].bitcast(FP8X4),
-                lhsT_scale=planes[:, k, :],
+                lhsT=operand[1][:, k, :].bitcast(FP8X4),
+                lhsT_scale=operand[2][:, k, :],
                 rhs=l_codes[:, k, :].bitcast(FP8X4),
                 rhs_scale=l_planes[:, k, :],
                 start=True,
@@ -116,18 +132,17 @@ def tile_butterflyblocksparselinear_e_kernel(
             source = bank[:].rearrange("p (a u e l) -> p u l a e", u=2, e=2, l=BLOCKS)
             target = hidden[:].rearrange("p l u (c e) -> p u l c e", e=2)
             for u in range(2):
-                nc.scalar.copy(out=target[:, u, :, 16 * k : 16 * (k + 1), :], in_=source[:, u])
+                copy(out=target[:, u, :, 16 * k : 16 * (k + 1), :], in_=source[:, u])
 
-        def second_product(operand, column_tile, half, result):
-            codes, planes = operand
+        def second_product(operand, half, column_tile, result):
             bank = psum.tile([P, BLOCK], F32, name="bank")
             by_block = bank[:].rearrange("p (j s) -> p j s", j=HALF)
             for j in range(HALF):
                 l = HALF * half + j
                 nc.tensor.matmul_mx(
                     out=by_block[:, j, :],
-                    lhsT=codes[:, l, :].bitcast(FP8X4),
-                    lhsT_scale=planes[:, l, :],
+                    lhsT=operand[1][:, l, :].bitcast(FP8X4),
+                    lhsT_scale=operand[2][:, l, :],
                     rhs=r_codes[:, l, PACK * P * column_tile : PACK * P * (column_tile + 1)].bitcast(FP8X4),
                     rhs_scale=r_planes[:, l, P * column_tile : P * (column_tile + 1)],
                     start=True,
@@ -135,38 +150,59 @@ def tile_butterflyblocksparselinear_e_kernel(
                 )
             these = slice(HALF * half, HALF * (half + 1))
             nc.vector.tensor_tensor(
-                out=result[:, :, these],
+                out=result[:, column_tile, :, these],
                 in0=bank[:].rearrange("p (j s) -> p s j", j=HALF),
                 in1=bias_by_column_tile[:, column_tile, :, these],
                 op=mybir.AluOpType.add,
             )
 
+
+        def live(half_tile):
+            return 0 <= half_tile < 2 * TILES
+
         x_operand = {}
         hidden_of = {}
         g_operand = {}
-        for step in range(TILES + 3):
-            if step < TILES:
-                x_pairs = tokens_of[step][:].bitcast(F32).rearrange("p (e c u) -> p e u c", e=BLOCKS, u=2)
-                x_operand[step] = make_operand(x_pairs, "x")
-            if 0 <= step - 2 < TILES:
-                g_operand[step - 2] = make_operand(hidden_of[step - 2][:].bitcast(F32), "g")
-            first = step - 1
-            second = step - 3
-            if 0 <= first < TILES:
-                hidden_of[first] = work.tile([P, BLOCKS, 2, 2 * P], BF16, name="hidden")
-            for column_tile in range(BLOCK // P):
-                if 0 <= second < TILES:
-                    result = results.tile([P, P, BLOCKS], F32, name="result")
-                for half in range(2):
-                    if 0 <= first < TILES:
-                        first_product(x_operand[first], hidden_of[first], 2 * column_tile + half)
-                    if 0 <= second < TILES:
-                        second_product(g_operand[second], column_tile, half, result)
-                if 0 <= second < TILES:
-                    nc.sync.dma_start(
-                        out=out_rows[
-                            P * second : P * (second + 1),
-                            BLOCKS * P * column_tile : BLOCKS * P * (column_tile + 1),
-                        ],
-                        in_=result[:].rearrange("p s l -> p (s l)"),
-                    )
+        result_of = {}
+        for this_round in range(ROUNDS):
+            to_transpose_x = this_round
+            to_multiply_first = this_round - FIRST_PRODUCT_LAG
+            to_transpose_h = this_round - HIDDEN_TRANSPOSE_LAG
+            to_multiply_second = this_round - SECOND_PRODUCT_LAG
+
+            if live(to_transpose_x):
+                i, half = divmod(to_transpose_x, 2)
+                if half == 0:
+                    x_operand[i] = new_operand("x")
+                x_pairs = tokens_of[i][:].bitcast(F32).rearrange("p (e c u) -> p e u c", e=BLOCKS, u=2)
+                transpose_half(x_pairs, x_operand[i], half, [nc.scalar.copy, nc.scalar.copy])
+            if live(to_transpose_h):
+                i, half = divmod(to_transpose_h, 2)
+                if half == 0:
+                    g_operand[i] = new_operand("g")
+                last_copy = nc.vector.tensor_copy if live(to_multiply_first) else nc.scalar.copy
+                transpose_half(hidden_of[i][:].bitcast(F32), g_operand[i], half, [nc.scalar.copy, last_copy])
+
+            for j in range(HALF):
+                if live(to_multiply_first):
+                    i, half = divmod(to_multiply_first, 2)
+                    if half == 0 and j == 0:
+                        hidden_of[i] = work.tile([P, BLOCKS, 2, 2 * P], BF16, name="hidden")
+                    spare_vector = not live(to_multiply_second) and j % 2 == 1
+                    copy = nc.vector.tensor_copy if spare_vector else nc.scalar.copy
+                    first_product(x_operand[i], hidden_of[i], HALF * half + j, copy)
+                if live(to_multiply_second):
+                    i, half = divmod(to_multiply_second, 2)
+                    if half == 0 and j == 0:
+                        result_of[i] = work.tile([P, BLOCK // P, P, BLOCKS], F32, name="result")
+                    second_product(g_operand[i], half, j, result_of[i])
+                    if half == 1:
+                        nc.sync.dma_start(
+                            out=out_rows[P * i : P * (i + 1), BLOCKS * P * j : BLOCKS * P * (j + 1)],
+                            in_=result_of[i][:, j].rearrange("p s l -> p (s l)"),
+                        )
+                if j == 0:
+                    if live(to_transpose_x):
+                        quantise_half(x_operand[to_transpose_x // 2], to_transpose_x % 2)
+                    if live(to_transpose_h):
+                        quantise_half(g_operand[to_transpose_h // 2], to_transpose_h % 2)

@@ -47,46 +47,51 @@ def tile_butterflyblocksparselinear_e_kernel(
         make_identity(nc, identity[:])
 
 
-        def load_tokens(i):
-            tokens = inputs.tile([P, WIDTH], BF16, name="tokens")
-            nc.sync.dma_start(out=tokens[:], in_=x_rows[P * i : P * (i + 1), :])
-            return tokens
-
-        def load_planes(scales, label):
-            planes = keep.tile([P, BLOCKS, BLOCK], U8, name=label + "_planes", align_bytes=64)
-            nc.vector.memset(planes[:].bitcast(I32), 0)
+        def load_factor(factor, words, scales, half):
+            codes, planes = factor
+            blocks = slice(HALF * half, HALF * (half + 1))
             scale_words = scales.bitcast(I32)
             for quadrant in range(QUADRANTS):
                 nc.sync.dma_start(
-                    out=planes[32 * quadrant : 32 * quadrant + 4].bitcast(I32),
-                    in_=scale_words[:, 4 * quadrant : 4 * quadrant + 4, :].rearrange("e r n -> r e n"),
+                    out=planes[32 * quadrant : 32 * quadrant + 16, half, :].bitcast(I32),
+                    in_=scale_words[blocks, 4 * quadrant : 4 * quadrant + 4, :],
                 )
-            return planes
-
-        def load_codes(codes, words, half):
-            blocks = slice(HALF * half, HALF * (half + 1))
             nc.sync.dma_start(
                 out=codes[:, blocks, :].bitcast(I32),
                 in_=words[blocks].rearrange("e p n t -> p e (n t)").bitcast(I32),
             )
 
-        l_codes = keep.tile([P, BLOCKS, PACK * BLOCK], U8, name="l_codes", align_bytes=64)
-        r_codes = keep.tile([P, BLOCKS, PACK * BLOCK], U8, name="r_codes", align_bytes=64)
+        def new_factor(label):
+            codes = keep.tile([P, BLOCKS, PACK * BLOCK], U8, name=label + "_codes", align_bytes=64)
+            planes = keep.tile([P, 2, BLOCK], U8, name=label + "_planes", align_bytes=64)
+            nc.vector.memset(planes[:].bitcast(I32), 0)
+            return codes, planes
+
+        factor_l = new_factor("l")
+        factor_r = new_factor("r")
         bias_rows = keep.tile([P, WIDTH], BF16, name="bias_rows")
         tokens_of = {}
-        tokens_of[0] = load_tokens(0)
-        l_planes = load_planes(factorL_scales, "l")
-        load_codes(l_codes, factorL_words, 0)
-        tokens_of[1] = load_tokens(1)
-        load_codes(l_codes, factorL_words, 1)
-        tokens_of[2] = load_tokens(2)
-        r_planes = load_planes(factorR_scales, "r")
-        load_codes(r_codes, factorR_words, 0)
-        nc.sync.dma_start(out=bias_rows[:], in_=bias.partition_broadcast(P))
-        load_codes(r_codes, factorR_words, 1)
-        for i in range(3, TILES):
-            tokens_of[i] = load_tokens(i)
+        for this_round in range(2 * TILES):
+            i, half = divmod(this_round, 2)
+            if half == 0:
+                tokens_of[i] = inputs.tile([P, WIDTH], BF16, name="tokens")
+                nc.sync.dma_start(out=tokens_of[i][:], in_=x_rows[P * i : P * (i + 1), :])
+            for factor_half in range(2):
+                if this_round == FIRST_PRODUCT_LAG + factor_half:
+                    load_factor(factor_l, factorL_words, factorL_scales, factor_half)
+                if this_round == SECOND_PRODUCT_LAG + factor_half:
+                    load_factor(factor_r, factorR_words, factorR_scales, factor_half)
+            if this_round == SECOND_PRODUCT_LAG:
+                nc.sync.dma_start(out=bias_rows[:], in_=bias.partition_broadcast(P))
         bias_by_column_tile = bias_rows[:].rearrange("p (c s l) -> p c s l", s=P, l=BLOCKS)
+
+        def factor_block(factor, e, first_column, columns):
+            codes, planes = factor
+            end_column = first_column + columns
+            return (
+                codes[:, e, PACK * first_column : PACK * end_column].bitcast(FP8X4),
+                planes[4 * (e % HALF) : P, e // HALF, first_column:end_column],
+            )
 
 
         def new_operand(label):
@@ -120,12 +125,13 @@ def tile_butterflyblocksparselinear_e_kernel(
 
         def first_product(operand, hidden, k, copy):
             bank = psum.tile([P, BLOCK], F32, name="bank")
+            rhs, rhs_scale = factor_block(factor_l, k, 0, BLOCK)
             nc.tensor.matmul_mx(
                 out=bank[:],
                 lhsT=operand[1][:, k, :].bitcast(FP8X4),
                 lhsT_scale=operand[2][:, k, :],
-                rhs=l_codes[:, k, :].bitcast(FP8X4),
-                rhs_scale=l_planes[:, k, :],
+                rhs=rhs,
+                rhs_scale=rhs_scale,
                 start=True,
                 stop=True,
             )
@@ -139,12 +145,13 @@ def tile_butterflyblocksparselinear_e_kernel(
             by_block = bank[:].rearrange("p (j s) -> p j s", j=HALF)
             for j in range(HALF):
                 l = HALF * half + j
+                rhs, rhs_scale = factor_block(factor_r, l, P * column_tile, P)
                 nc.tensor.matmul_mx(
                     out=by_block[:, j, :],
                     lhsT=operand[1][:, l, :].bitcast(FP8X4),
                     lhsT_scale=operand[2][:, l, :],
-                    rhs=r_codes[:, l, PACK * P * column_tile : PACK * P * (column_tile + 1)].bitcast(FP8X4),
-                    rhs_scale=r_planes[:, l, P * column_tile : P * (column_tile + 1)],
+                    rhs=rhs,
+                    rhs_scale=rhs_scale,
                     start=True,
                     stop=True,
                 )

@@ -25,6 +25,7 @@ FIRST_PRODUCT_LAG = 1
 HIDDEN_TRANSPOSE_LAG = 3
 SECOND_PRODUCT_LAG = 4
 ROUNDS = 2 * TILES + SECOND_PRODUCT_LAG
+BIAS_BANKS_A_ROUND = WIDTH // BLOCK // SECOND_PRODUCT_LAG
 
 FLOPS = 2 * 2 * TOKENS * BLOCKS * BLOCK * BLOCK
 
@@ -46,6 +47,10 @@ def tile_butterflyblocksparselinear_e_kernel(
         identity = keep.tile([P, P], F32, name="identity")
         make_identity(nc, identity[:])
 
+
+        def load_tokens(tokens, i, half):
+            columns = slice(HALF * BLOCK * half, HALF * BLOCK * (half + 1))
+            nc.sync.dma_start(out=tokens[:, columns], in_=x_rows[P * i : P * (i + 1), columns])
 
         def load_factor(factor, words, scales, half):
             codes, planes = factor
@@ -69,21 +74,33 @@ def tile_butterflyblocksparselinear_e_kernel(
 
         factor_l = new_factor("l")
         factor_r = new_factor("r")
-        bias_rows = keep.tile([P, WIDTH], BF16, name="bias_rows")
+        bias_row = keep.tile([P, WIDTH], BF16, name="bias_row")
+        nc.vector.memset(bias_row[:].bitcast(I32), 0)
         tokens_of = {}
         for this_round in range(2 * TILES):
             i, half = divmod(this_round, 2)
             if half == 0:
                 tokens_of[i] = inputs.tile([P, WIDTH], BF16, name="tokens")
-                nc.sync.dma_start(out=tokens_of[i][:], in_=x_rows[P * i : P * (i + 1), :])
+            load_tokens(tokens_of[i], i, half)
             for factor_half in range(2):
                 if this_round == FIRST_PRODUCT_LAG + factor_half:
                     load_factor(factor_l, factorL_words, factorL_scales, factor_half)
                 if this_round == SECOND_PRODUCT_LAG + factor_half:
                     load_factor(factor_r, factorR_words, factorR_scales, factor_half)
-            if this_round == SECOND_PRODUCT_LAG:
-                nc.sync.dma_start(out=bias_rows[:], in_=bias.partition_broadcast(P))
+            if this_round == 0:
+                nc.sync.dma_start(out=bias_row[0:1, :], in_=bias.rearrange("(o n) -> o n", o=1))
+
+        ones = keep.tile([P, P], BF16, name="ones")
+        nc.vector.memset(ones[:], 1.0)
+        bias_rows = keep.tile([P, WIDTH], BF16, name="bias_rows")
         bias_by_column_tile = bias_rows[:].rearrange("p (c s l) -> p c s l", s=P, l=BLOCKS)
+
+        def spread_bias(first_bank, banks):
+            for b in range(first_bank, first_bank + banks):
+                columns = slice(BLOCK * b, BLOCK * (b + 1))
+                bank = psum.tile([P, BLOCK], F32, name="bank")
+                nc.tensor.matmul(out=bank[:], lhsT=ones[:], rhs=bias_row[:, columns], start=True, stop=True)
+                nc.vector.tensor_copy(out=bias_rows[:, columns], in_=bank[:])
 
         def factor_block(factor, e, first_column, columns):
             codes, planes = factor
@@ -189,6 +206,9 @@ def tile_butterflyblocksparselinear_e_kernel(
                     g_operand[i] = new_operand("g")
                 last_copy = nc.vector.tensor_copy if live(to_multiply_first) else nc.scalar.copy
                 transpose_half(hidden_of[i][:].bitcast(F32), g_operand[i], half, [nc.scalar.copy, last_copy])
+
+            if this_round < SECOND_PRODUCT_LAG:
+                spread_bias(BIAS_BANKS_A_ROUND * this_round, BIAS_BANKS_A_ROUND)
 
             for j in range(HALF):
                 if live(to_multiply_first):

@@ -111,13 +111,13 @@ def tile_butterflyblocksparselinear_e_kernel(
             )
 
 
-        def new_operand(label):
-            grouped = work.tile([P, BLOCKS, P, PACK], BF16, name=label + "_grouped", align_bytes=64)
-            codes = work.tile([P, BLOCKS, P], U32, name=label + "_codes", align_bytes=64)
-            planes = work.tile([P, BLOCKS, P], U8, name=label + "_planes", align_bytes=64)
+        def new_operand():
+            grouped = work.tile([P, 2, HALF, P, PACK], BF16, name="grouped", align_bytes=64)
+            codes = work.tile([P, 2, HALF, P], U32, name="codes", align_bytes=64)
+            planes = work.tile([P, 2, HALF, P], U8, name="planes", align_bytes=64)
             return grouped, codes, planes
 
-        def transpose_half(pairs, operand, half, copies):
+        def transpose_half(pairs, operand, stage, half, copies):
             grouped_words = operand[0][:].bitcast(F32)
             for b in range(HALF // 2):
                 first_block = HALF * half + 2 * b
@@ -127,17 +127,17 @@ def tile_butterflyblocksparselinear_e_kernel(
                     for u in range(2):
                         nc.tensor.transpose(by_plane[:, j, u, :], pairs[:, first_block + j, u, :], identity[:])
                 copies[b](
-                    out=grouped_words[:, first_block : first_block + 2],
+                    out=grouped_words[:, stage, 2 * b : 2 * b + 2],
                     in_=bank[:].rearrange("p (j u n) -> p j n u", j=2, u=2),
                 )
 
-        def quantise_half(operand, half):
+        def quantise(operand, first_stage, stages):
             grouped, codes, planes = operand
-            blocks = slice(HALF * half, HALF * (half + 1))
+            these = slice(first_stage, first_stage + stages)
             nc.vector.quantize_mx(
-                out=codes[:, blocks, :].rearrange("p e n -> p (e n)").bitcast(FP8X4),
-                scales=planes[:, blocks, :].rearrange("p e n -> p (e n)"),
-                in_=grouped[:, blocks].rearrange("p e n t -> p (e n t)"),
+                out=codes[:, these].rearrange("p g e n -> p (g e n)").bitcast(FP8X4),
+                scales=planes[:, these].rearrange("p g e n -> p (g e n)"),
+                in_=grouped[:, these].rearrange("p g e n t -> p (g e n t)"),
             )
 
         def first_product(operand, hidden, k, copy):
@@ -145,8 +145,8 @@ def tile_butterflyblocksparselinear_e_kernel(
             rhs, rhs_scale = factor_block(factor_l, k, 0, BLOCK)
             nc.tensor.matmul_mx(
                 out=bank[:],
-                lhsT=operand[1][:, k, :].bitcast(FP8X4),
-                lhsT_scale=operand[2][:, k, :],
+                lhsT=operand[1][:, 0, k % HALF, :].bitcast(FP8X4),
+                lhsT_scale=operand[2][:, 0, k % HALF, :],
                 rhs=rhs,
                 rhs_scale=rhs_scale,
                 start=True,
@@ -165,8 +165,8 @@ def tile_butterflyblocksparselinear_e_kernel(
                 rhs, rhs_scale = factor_block(factor_r, l, P * column_tile, P)
                 nc.tensor.matmul_mx(
                     out=by_block[:, j, :],
-                    lhsT=operand[1][:, l, :].bitcast(FP8X4),
-                    lhsT_scale=operand[2][:, l, :],
+                    lhsT=operand[1][:, 1, j, :].bitcast(FP8X4),
+                    lhsT_scale=operand[2][:, 1, j, :],
                     rhs=rhs,
                     rhs_scale=rhs_scale,
                     start=True,
@@ -184,9 +184,8 @@ def tile_butterflyblocksparselinear_e_kernel(
         def live(half_tile):
             return 0 <= half_tile < 2 * TILES
 
-        x_operand = {}
+        operand_of = {}
         hidden_of = {}
-        g_operand = {}
         result_of = {}
         for this_round in range(ROUNDS):
             to_transpose_x = this_round
@@ -194,18 +193,16 @@ def tile_butterflyblocksparselinear_e_kernel(
             to_transpose_h = this_round - HIDDEN_TRANSPOSE_LAG
             to_multiply_second = this_round - SECOND_PRODUCT_LAG
 
+            if live(to_transpose_x) or live(to_transpose_h):
+                operand_of[this_round] = new_operand()
             if live(to_transpose_x):
                 i, half = divmod(to_transpose_x, 2)
-                if half == 0:
-                    x_operand[i] = new_operand("x")
                 x_pairs = tokens_of[i][:].bitcast(F32).rearrange("p (e c u) -> p e u c", e=BLOCKS, u=2)
-                transpose_half(x_pairs, x_operand[i], half, [nc.scalar.copy, nc.scalar.copy])
+                transpose_half(x_pairs, operand_of[this_round], 0, half, [nc.scalar.copy, nc.scalar.copy])
             if live(to_transpose_h):
                 i, half = divmod(to_transpose_h, 2)
-                if half == 0:
-                    g_operand[i] = new_operand("g")
                 last_copy = nc.vector.tensor_copy if live(to_multiply_first) else nc.scalar.copy
-                transpose_half(hidden_of[i][:].bitcast(F32), g_operand[i], half, [nc.scalar.copy, last_copy])
+                transpose_half(hidden_of[i][:].bitcast(F32), operand_of[this_round], 1, half, [nc.scalar.copy, last_copy])
 
             if this_round < SECOND_PRODUCT_LAG:
                 spread_bias(BIAS_BANKS_A_ROUND * this_round, BIAS_BANKS_A_ROUND)
@@ -217,19 +214,21 @@ def tile_butterflyblocksparselinear_e_kernel(
                         hidden_of[i] = work.tile([P, BLOCKS, 2, 2 * P], BF16, name="hidden")
                     spare_vector = not live(to_multiply_second) and j % 2 == 1
                     copy = nc.vector.tensor_copy if spare_vector else nc.scalar.copy
-                    first_product(x_operand[i], hidden_of[i], HALF * half + j, copy)
+                    first_product(operand_of[this_round - 1], hidden_of[i], HALF * half + j, copy)
                 if live(to_multiply_second):
                     i, half = divmod(to_multiply_second, 2)
                     if half == 0 and j == 0:
                         result_of[i] = work.tile([P, BLOCK // P, P, BLOCKS], F32, name="result")
-                    second_product(g_operand[i], half, j, result_of[i])
+                    second_product(operand_of[this_round - 1], half, j, result_of[i])
                     if half == 1:
                         nc.sync.dma_start(
                             out=out_rows[P * i : P * (i + 1), BLOCKS * P * j : BLOCKS * P * (j + 1)],
                             in_=result_of[i][:, j].rearrange("p s l -> p (s l)"),
                         )
                 if j == 0:
-                    if live(to_transpose_x):
-                        quantise_half(x_operand[to_transpose_x // 2], to_transpose_x % 2)
-                    if live(to_transpose_h):
-                        quantise_half(g_operand[to_transpose_h // 2], to_transpose_h % 2)
+                    if live(to_transpose_x) and live(to_transpose_h):
+                        quantise(operand_of[this_round], 0, 2)
+                    elif live(to_transpose_x):
+                        quantise(operand_of[this_round], 0, 1)
+                    elif live(to_transpose_h):
+                        quantise(operand_of[this_round], 1, 1)

@@ -41,6 +41,7 @@ def tile_butterflyblocksparselinear_e_kernel(
         keep = ctx.enter_context(tc.tile_pool(name="keep", bufs=1))
         inputs = ctx.enter_context(tc.tile_pool(name="inputs", bufs=TILES))
         work = ctx.enter_context(tc.tile_pool(name="work", bufs=2))
+        results = ctx.enter_context(tc.tile_pool(name="results", bufs=4))
         psum = ctx.enter_context(tc.psum_pool(name="psum", bufs=PSUM_BANKS))
         ctx.enter_context(tc.manual_schedule())
 
@@ -218,7 +219,7 @@ def tile_butterflyblocksparselinear_e_kernel(
                 if live(to_multiply_second):
                     i, half = divmod(to_multiply_second, 2)
                     if half == 0 and j == 0:
-                        result_of[i] = work.tile([P, BLOCK // P, P, BLOCKS], F32, name="result")
+                        result_of[i] = results.tile([P, BLOCK // P, P, BLOCKS], F32, name="result")
                     second_product(operand_of[this_round - 1], half, j, result_of[i])
                     if half == 1:
                         nc.sync.dma_start(

@@ -50,8 +50,12 @@ def tile_butterflyblocksparselinear_e_kernel(
 
 
         def load_tokens(tokens, i, half):
-            columns = slice(HALF * BLOCK * half, HALF * BLOCK * (half + 1))
-            nc.sync.dma_start(out=tokens[:, columns], in_=x_rows[P * i : P * (i + 1), columns])
+            pieces = 2 if i == 0 and half == 0 else 1
+            width = HALF * BLOCK // pieces
+            for piece in range(pieces):
+                first = HALF * BLOCK * half + width * piece
+                columns = slice(first, first + width)
+                nc.sync.dma_start(out=tokens[:, columns], in_=x_rows[P * i : P * (i + 1), columns])
 
         def load_factor(factor, words, scales, half):
             codes, planes = factor
@@ -83,13 +87,13 @@ def tile_butterflyblocksparselinear_e_kernel(
             if half == 0:
                 tokens_of[i] = inputs.tile([P, WIDTH], BF16, name="tokens")
             load_tokens(tokens_of[i], i, half)
+            if this_round == 1:
+                nc.sync.dma_start(out=bias_row[0:1, :], in_=bias.rearrange("(o n) -> o n", o=1))
             for factor_half in range(2):
                 if this_round == FIRST_PRODUCT_LAG + factor_half:
                     load_factor(factor_l, factorL_words, factorL_scales, factor_half)
                 if this_round == SECOND_PRODUCT_LAG + factor_half:
                     load_factor(factor_r, factorR_words, factorR_scales, factor_half)
-            if this_round == 0:
-                nc.sync.dma_start(out=bias_row[0:1, :], in_=bias.rearrange("(o n) -> o n", o=1))
 
         ones = keep.tile([P, P], BF16, name="ones")
         nc.vector.memset(ones[:], 1.0)

from contextlib import ExitStack

import concourse.mybir as mybir
from concourse.masks import make_identity

F32 = mybir.dt.float32
BF16 = mybir.dt.bfloat16
I32 = mybir.dt.int32
U32 = mybir.dt.uint32
U8 = mybir.dt.uint8
FP8X4 = mybir.dt.float8_e4m3fn_x4

P = 128
PACK = 4
BLOCKS = 8
BLOCK = P * PACK
TOKENS = 1024
WIDTH = BLOCKS * BLOCK
TILES = TOKENS // P
PSUM_BANKS = 8
QUADRANTS = 4
HALF = BLOCKS // 2

FIRST_PRODUCT_LAG = 1
HIDDEN_TRANSPOSE_LAG = 3
SECOND_PRODUCT_LAG = 4
ROUNDS = 2 * TILES + SECOND_PRODUCT_LAG
BIAS_BANKS_A_ROUND = WIDTH // BLOCK // SECOND_PRODUCT_LAG

FLOPS = 2 * 2 * TOKENS * BLOCKS * BLOCK * BLOCK


def tile_butterflyblocksparselinear_e_kernel(
    tc, x, factorL_words, factorL_scales, factorR_words, factorR_scales, bias, out
):
    nc = tc.nc
    x_rows = x.flatten_outer_dims()
    out_rows = out.flatten_outer_dims()

    with ExitStack() as ctx:
        keep = ctx.enter_context(tc.tile_pool(name="keep", bufs=1))
        inputs = ctx.enter_context(tc.tile_pool(name="inputs", bufs=TILES))
        work = ctx.enter_context(tc.tile_pool(name="work", bufs=2))
        results = ctx.enter_context(tc.tile_pool(name="results", bufs=4))
        psum = ctx.enter_context(tc.psum_pool(name="psum", bufs=PSUM_BANKS))
        ctx.enter_context(tc.manual_schedule())

        identity = keep.tile([P, P], F32, name="identity")
        make_identity(nc, identity[:])


        def load_tokens(tokens, i, half):
            pieces = 2 if i == 0 and half == 0 else 1
            width = HALF * BLOCK // pieces
            for piece in range(pieces):
                first = HALF * BLOCK * half + width * piece
                columns = slice(first, first + width)
                nc.sync.dma_start(out=tokens[:, columns], in_=x_rows[P * i : P * (i + 1), columns])

        def load_factor(factor, words, scales, half):
            codes, planes = factor
            blocks = slice(HALF * half, HALF * (half + 1))
            scale_words = scales.bitcast(I32)
            for quadrant in range(QUADRANTS):
                nc.sync.dma_start(
                    out=planes[32 * quadrant : 32 * quadrant + 16, half, :].bitcast(I32),
                    in_=scale_words[blocks, 4 * quadrant : 4 * quadrant + 4, :],
                )
            nc.sync.dma_start(
                out=codes[:, blocks, :].bitcast(I32),
                in_=words[blocks].rearrange("e p n t -> p e (n t)").bitcast(I32),
            )

        def new_factor(label):
            codes = keep.tile([P, BLOCKS, PACK * BLOCK], U8, name=label + "_codes", align_bytes=64)
            planes = keep.tile([P, 2, BLOCK], U8, name=label + "_planes", align_bytes=64)
            nc.vector.memset(planes[:].bitcast(I32), 0)
            return codes, planes

        factor_l = new_factor("l")
        factor_r = new_factor("r")
        bias_row = keep.tile([P, WIDTH], BF16, name="bias_row")
        nc.vector.memset(bias_row[:].bitcast(I32), 0)
        tokens_of = {}
        for this_round in range(2 * TILES):
            i, half = divmod(this_round, 2)
            if half == 0:
                tokens_of[i] = inputs.tile([P, WIDTH], BF16, name="tokens")
            load_tokens(tokens_of[i], i, half)
            if this_round == 1:
                nc.sync.dma_start(out=bias_row[0:1, :], in_=bias.rearrange("(o n) -> o n", o=1))
            for factor_half in range(2):
                if this_round == FIRST_PRODUCT_LAG + factor_half:
                    load_factor(factor_l, factorL_words, factorL_scales, factor_half)
                if this_round == SECOND_PRODUCT_LAG + factor_half:
                    load_factor(factor_r, factorR_words, factorR_scales, factor_half)

        ones = keep.tile([P, P], BF16, name="ones")
        nc.vector.memset(ones[:], 1.0)
        bias_rows = keep.tile([P, WIDTH], BF16, name="bias_rows")
        bias_by_column_tile = bias_rows[:].rearrange("p (c s l) -> p c s l", s=P, l=BLOCKS)

        def spread_bias(first_bank, banks):
            for b in range(first_bank, first_bank + banks):
                columns = slice(BLOCK * b, BLOCK * (b + 1))
                bank = psum.tile([P, BLOCK], F32, name="bank")
                nc.tensor.matmul(out=bank[:], lhsT=ones[:], rhs=bias_row[:, columns], start=True, stop=True)
                nc.vector.tensor_copy(out=bias_rows[:, columns], in_=bank[:])

        def factor_block(factor, e, first_column, columns):
            codes, planes = factor
            end_column = first_column + columns
            return (
                codes[:, e, PACK * first_column : PACK * end_column].bitcast(FP8X4),
                planes[4 * (e % HALF) : P, e // HALF, first_column:end_column],
            )


        def new_operand():
            grouped = work.tile([P, 2, HALF, P, PACK], BF16, name="grouped", align_bytes=64)
            codes = work.tile([P, 2, HALF, P], U32, name="codes", align_bytes=64)
            planes = work.tile([P, 2, HALF, P], U8, name="planes", align_bytes=64)
            return grouped, codes, planes

        def transpose_half(pairs, operand, stage, half, copies):
            grouped_words = operand[0][:].bitcast(F32)
            for b in range(HALF // 2):
                first_block = HALF * half + 2 * b
                bank = psum.tile([P, BLOCK], F32, name="bank")
                by_plane = bank[:].rearrange("p (j u n) -> p j u n", j=2, u=2)
                for j in range(2):
                    for u in range(2):
                        nc.tensor.transpose(by_plane[:, j, u, :], pairs[:, first_block + j, u, :], identity[:])
                copies[b](
                    out=grouped_words[:, stage, 2 * b : 2 * b + 2],
                    in_=bank[:].rearrange("p (j u n) -> p j n u", j=2, u=2),
                )

        def quantise(operand, first_stage, stages):
            grouped, codes, planes = operand
            these = slice(first_stage, first_stage + stages)
            nc.vector.quantize_mx(
                out=codes[:, these].rearrange("p g e n -> p (g e n)").bitcast(FP8X4),
                scales=planes[:, these].rearrange("p g e n -> p (g e n)"),
                in_=grouped[:, these].rearrange("p g e n t -> p (g e n t)"),
            )

        def first_product(operand, hidden, k, copy):
            bank = psum.tile([P, BLOCK], F32, name="bank")
            rhs, rhs_scale = factor_block(factor_l, k, 0, BLOCK)
            nc.tensor.matmul_mx(
                out=bank[:],
                lhsT=operand[1][:, 0, k % HALF, :].bitcast(FP8X4),
                lhsT_scale=operand[2][:, 0, k % HALF, :],
                rhs=rhs,
                rhs_scale=rhs_scale,
                start=True,
                stop=True,
            )
            source = bank[:].rearrange("p (a u e l) -> p u l a e", u=2, e=2, l=BLOCKS)
            target = hidden[:].rearrange("p l u (c e) -> p u l c e", e=2)
            for u in range(2):
                copy(out=target[:, u, :, 16 * k : 16 * (k + 1), :], in_=source[:, u])

        def second_product(operand, half, column_tile, result):
            bank = psum.tile([P, BLOCK], F32, name="bank")
            by_block = bank[:].rearrange("p (j s) -> p j s", j=HALF)
            for j in range(HALF):
                l = HALF * half + j
                rhs, rhs_scale = factor_block(factor_r, l, P * column_tile, P)
                nc.tensor.matmul_mx(
                    out=by_block[:, j, :],
                    lhsT=operand[1][:, 1, j, :].bitcast(FP8X4),
                    lhsT_scale=operand[2][:, 1, j, :],
                    rhs=rhs,
                    rhs_scale=rhs_scale,
                    start=True,
                    stop=True,
                )
            these = slice(HALF * half, HALF * (half + 1))
            nc.vector.tensor_tensor(
                out=result[:, column_tile, :, these],
                in0=bank[:].rearrange("p (j s) -> p s j", j=HALF),
                in1=bias_by_column_tile[:, column_tile, :, these],
                op=mybir.AluOpType.add,
            )


        def live(half_tile):
            return 0 <= half_tile < 2 * TILES

        operand_of = {}
        hidden_of = {}
        result_of = {}
        for this_round in range(ROUNDS):
            to_transpose_x = this_round
            to_multiply_first = this_round - FIRST_PRODUCT_LAG
            to_transpose_h = this_round - HIDDEN_TRANSPOSE_LAG
            to_multiply_second = this_round - SECOND_PRODUCT_LAG

            if live(to_transpose_x) or live(to_transpose_h):
                operand_of[this_round] = new_operand()
            if live(to_transpose_x):
                i, half = divmod(to_transpose_x, 2)
                x_pairs = tokens_of[i][:].bitcast(F32).rearrange("p (e c u) -> p e u c", e=BLOCKS, u=2)
                transpose_half(x_pairs, operand_of[this_round], 0, half, [nc.scalar.copy, nc.scalar.copy])
            if live(to_transpose_h):
                i, half = divmod(to_transpose_h, 2)
                last_copy = nc.vector.tensor_copy if live(to_multiply_first) else nc.scalar.copy
                transpose_half(hidden_of[i][:].bitcast(F32), operand_of[this_round], 1, half, [nc.scalar.copy, last_copy])

            if this_round < SECOND_PRODUCT_LAG:
                spread_bias(BIAS_BANKS_A_ROUND * this_round, BIAS_BANKS_A_ROUND)

            for j in range(HALF):
                if live(to_multiply_first):
                    i, half = divmod(to_multiply_first, 2)
                    if half == 0 and j == 0:
                        hidden_of[i] = work.tile([P, BLOCKS, 2, 2 * P], BF16, name="hidden")
                    spare_vector = not live(to_multiply_second) and j % 2 == 1
                    copy = nc.vector.tensor_copy if spare_vector else nc.scalar.copy
                    first_product(operand_of[this_round - 1], hidden_of[i], HALF * half + j, copy)
                if live(to_multiply_second):
                    i, half = divmod(to_multiply_second, 2)
                    if half == 0 and j == 0:
                        result_of[i] = results.tile([P, BLOCK // P, P, BLOCKS], F32, name="result")
                    second_product(operand_of[this_round - 1], half, j, result_of[i])
                    if half == 1:
                        nc.sync.dma_start(
                            out=out_rows[P * i : P * (i + 1), BLOCKS * P * j : BLOCKS * P * (j + 1)],
                            in_=result_of[i][:, j].rearrange("p s l -> p (s l)"),
                        )
                if j == 0:
                    if live(to_transpose_x) and live(to_transpose_h):
                        quantise(operand_of[this_round], 0, 2)
                    elif live(to_transpose_x):
                        quantise(operand_of[this_round], 0, 1)
                    elif live(to_transpose_h):
                        quantise(operand_of[this_round], 1, 1)
